import numpy as np
import ml_dtypes


def mxq(x, axis, fmt="e4m3"):
    dtype, down = {"e4m3": (ml_dtypes.float8_e4m3fn, 7), "e5m2": (ml_dtypes.float8_e5m2, 14)}[fmt]
    v = np.moveaxis(np.asarray(x, np.float32).astype(ml_dtypes.bfloat16).astype(np.float64), axis, -1)
    blocks = v.reshape(v.shape[:-1] + (-1, 32))
    amax = np.abs(blocks).max(-1, keepdims=True)
    byte = np.maximum(np.where(amax > 0, np.frexp(amax)[1] - 1 + 127, 0) - down, 1)
    scale = np.exp2(byte - 127.0)
    codes = (blocks / scale).astype(np.float32).astype(dtype).astype(np.float64)
    return np.moveaxis((codes * scale).reshape(v.shape), -1, axis)


WIDE = False


def mx_kscale(k):
    if not WIDE:
        return np.ones(k)
    levels = np.array([10, -10, 5, -5, 0])
    a = np.random.permutation(np.resize(levels, k // 512 * 4)).reshape(k // 512, 4)
    idx = np.arange(k)
    return np.exp2(a[idx // 512, idx % 128 // 32])


BF16 = ml_dtypes.bfloat16


def bf(x):
    return np.asarray(x, np.float32).astype(BF16)


def f64(x):
    return np.asarray(x).astype(np.float64)


B, H, S, D = 1, 4, 1024, 512
C = 1.0
TAU = 1.0
EPS = 1e-7
R2 = 0.5


def arccosh(a):
    return np.log(a + np.sqrt(a * a - 1.0))


def poincare_dist2(q, k, c):
    qn = np.sum(q * q, axis=-1)
    kn = np.sum(k * k, axis=-1)
    qk = q @ k.transpose(0, 1, 3, 2)
    diff2 = np.maximum(qn[..., :, None] + kn[..., None, :] - 2.0 * qk, 0.0)
    denom = (1.0 - c * qn)[..., :, None] * (1.0 - c * kn)[..., None, :]
    arg = 1.0 + 2.0 * c * diff2 / np.maximum(denom, EPS)
    d = arccosh(np.maximum(arg, 1.0 + EPS)) / np.sqrt(c)
    return d * d


def setup_inputs():
    s = mx_kscale(S)
    a = np.log2(s / s.min())
    q = np.random.standard_normal((B, H, S, D)) * np.sqrt(R2 / D)
    k0 = np.random.standard_normal((B, H, S, D)) * np.sqrt(R2 / D)
    v = np.random.standard_normal((B, H, S, D)) * 0.125 * np.sqrt(S)
    kn0 = np.sum(k0 * k0, axis=-1)
    arg0 = 1.0 + 2.0 * C * (R2 + kn0) / ((1.0 - C * R2) * (1.0 - C * kn0))
    t = arccosh(arg0) ** 2 / C + a * np.log(2.0) * TAU
    g = (np.cosh(np.sqrt(C * t)) - 1.0) * (1.0 - C * R2) / (2.0 * C)
    r2 = (g - R2) / (1.0 + C * g)
    k = k0 * np.sqrt(r2 / kn0)[..., None]
    return {"query_states": bf(q), "key_states": bf(k), "value_states": bf(v * (2.0 ** a)[:, None])}


def reference(query_states, key_states, value_states):
    scores = -poincare_dist2(f64(query_states), f64(key_states), C) / TAU
    e = np.exp(scores - scores.max(-1, keepdims=True))
    return (mxq(e, 3, "e4m3") @ mxq(f64(value_states), 2, "e4m3")) / e.sum(-1, keepdims=True)

@@ -1,0 +1,298 @@
+from contextlib import ExitStack
+
+import concourse.mybir as mybir
+from concourse.masks import make_identity
+
+F32 = mybir.dt.float32
+BF16 = mybir.dt.bfloat16
+U32 = mybir.dt.uint32
+U8 = mybir.dt.uint8
+FP8X4 = mybir.dt.float8_e4m3fn_x4
+ALU = mybir.AluOpType
+FUNC = mybir.ActivationFunctionType
+
+P = 128
+HEADS = 4
+SEQ = 1024
+FEAT = 512
+TILES = SEQ // P
+CHUNKS = FEAT // P
+BANK = 512
+HALVES = SEQ // BANK
+PACK = 4
+PASSES = SEQ // (P * PACK)
+EPS = 1e-7
+TINY = 1e-10
+CHAIN = 3
+FLOPS = 2 * 2 * HEADS * SEQ * SEQ * FEAT
+
+
+def tile_riemannianattention_t_kernel(tc, query_states, key_states, value_states, out):
+    nc = tc.nc
+    q_rows = query_states.flatten_outer_dims()
+    k_rows = key_states.flatten_outer_dims()
+    v_rows = value_states.flatten_outer_dims()
+    out_rows = out.flatten_outer_dims()
+
+    with ExitStack() as stack:
+        keep = stack.enter_context(tc.tile_pool(name="keep", bufs=1))
+        natural = stack.enter_context(tc.tile_pool(name="natural", bufs=2))
+        flipped = stack.enter_context(tc.tile_pool(name="flipped", bufs=2))
+        spread = stack.enter_context(tc.tile_pool(name="spread", bufs=2))
+        values = stack.enter_context(tc.tile_pool(name="values", bufs=1))
+        rows = stack.enter_context(tc.tile_pool(name="rows", bufs=TILES + 6))
+        work = stack.enter_context(tc.tile_pool(name="work", bufs=3))
+        score_banks = stack.enter_context(tc.psum_pool(name="score_banks", bufs=4))
+        flip_banks = stack.enter_context(tc.psum_pool(name="flip_banks", bufs=2))
+        out_banks = stack.enter_context(tc.psum_pool(name="out_banks", bufs=2))
+
+        ident_b = keep.tile([P, P], BF16, name="ident_b")
+        make_identity(nc, ident_b[:])
+        ident_f = keep.tile([P, P], F32, name="ident_f")
+        make_identity(nc, ident_f[:])
+
+        stack.enter_context(tc.manual_schedule())
+
+        k_nat, q_nat, k_flip, q_flip, v_raw = {}, {}, {}, {}, {}
+        v_codes, v_scales = {}, {}
+        small = {}
+        wide = {}
+        ratio = {}
+        product = {}
+        e_bf, e_flip, e_grp, e_codes, e_scales, pv = {}, {}, {}, {}, {}, {}
+
+        def head_rows(dram, h):
+            return dram[h * SEQ : (h + 1) * SEQ, :]
+
+        def load_qk(h):
+            k_nat[h] = natural.tile([P, TILES, FEAT], BF16, name="k_nat")
+            nc.sync.dma_start(
+                out=k_nat[h][:].rearrange("p (g t) d -> p g (t d)", g=PASSES),
+                in_=head_rows(k_rows, h).rearrange("(g p t) d -> p g (t d)", g=PASSES, p=P),
+            )
+            q_nat[h] = natural.tile([P, TILES, FEAT], BF16, name="q_nat")
+            nc.sync.dma_start(
+                out=q_nat[h][:].rearrange("p r d -> p (r d)"),
+                in_=head_rows(q_rows, h).rearrange("(p r) d -> p (r d)", p=P),
+            )
+            small[h] = {}
+            for name in ("kn", "qn", "rowsum"):
+                small[h][name] = keep.tile([P, TILES], F32, name="%s_%d" % (name, h))
+
+        def load_v(h):
+            v_raw[h] = values.tile([P, PASSES, PACK, FEAT], BF16, name="v_raw")
+            nc.sync.dma_start(
+                out=v_raw[h][:].rearrange("p g t d -> p g (t d)"),
+                in_=head_rows(v_rows, h).rearrange("(g p t) d -> p g (t d)", g=PASSES, p=P),
+            )
+
+        def quantise_v(h):
+            v_grp = values.tile([P, PASSES, FEAT, PACK], BF16, name="v_grp", align_bytes=64)
+            for g in range(PASSES):
+                nc.vector.tensor_copy(out=v_grp[:, g], in_=v_raw[h][:, g].rearrange("p t d -> p d t"))
+            v_codes[h] = keep.tile([P, PASSES, FEAT], U32, name="v_codes_%d" % h, align_bytes=64)
+            v_scales[h] = keep.tile([P, PASSES, FEAT], U8, name="v_scales_%d" % h, align_bytes=64)
+            nc.vector.quantize_mx(
+                out=v_codes[h][:].rearrange("p g d -> p (g d)").bitcast(FP8X4),
+                scales=v_scales[h][:].rearrange("p g d -> p (g d)"),
+                in_=v_grp[:].rearrange("p g d t -> p (g d t)"),
+            )
+
+        def norms_and_flip(h, step, copy_out):
+            if step == 0:
+                k_flip[h] = flipped.tile([P, CHUNKS, SEQ], BF16, name="k_flip")
+                q_flip[h] = flipped.tile([P, CHUNKS, SEQ], BF16, name="q_flip")
+            for nat, name in ((k_nat[h], "kn"), (q_nat[h], "qn")):
+                squares = work.tile([P, FEAT], BF16, name="squares")
+                nc.scalar.activation(
+                    out=squares[:],
+                    in_=nat[:, step, :],
+                    func=FUNC.Square,
+                    accum_out=small[h][name][:, step : step + 1],
+                )
+            nat, flip = (k_nat[h], k_flip[h]) if step < CHUNKS else (q_nat[h], q_flip[h])
+            c = step % CHUNKS
+            bank = flip_banks.tile([P, SEQ], BF16, name="bank", tag="flip")
+            for r in range(TILES):
+                nc.tensor.transpose(bank[:, r * P : (r + 1) * P], nat[:, r, c * P : (c + 1) * P], ident_b[:])
+            copy_out(out=flip[:, c, :], in_=bank[:])
+
+        def per_row_values(h):
+            s = small[h]
+            for name in ("k_gap", "k_weight", "k_half", "q_gap", "q_inv", "q_inv2", "q_half", "q_cap", "q_floor", "rinv"):
+                s[name] = keep.tile([P, TILES], F32, name="%s_%d" % (name, h))
+            for norm, gap in (("kn", "k_gap"), ("qn", "q_gap")):
+                nc.vector.tensor_scalar(out=s[gap][:], in0=s[norm][:], scalar1=-1.0, scalar2=1.0, op0=ALU.mult, op1=ALU.add)
+                nc.vector.tensor_scalar_max(out=s[gap][:], in0=s[gap][:], scalar1=TINY)
+            nc.vector.reciprocal(out=s["k_weight"][:], in_=s["k_gap"][:])
+            nc.vector.tensor_scalar_mul(out=s["k_weight"][:], in0=s["k_weight"][:], scalar1=-2.0)
+            nc.vector.tensor_scalar_mul(out=s["k_half"][:], in0=s["kn"][:], scalar1=0.5)
+            nc.vector.reciprocal(out=s["q_inv"][:], in_=s["q_gap"][:])
+            nc.vector.tensor_mul(out=s["q_inv2"][:], in0=s["q_inv"][:], in1=s["q_inv"][:])
+            nc.vector.tensor_scalar_mul(out=s["q_half"][:], in0=s["qn"][:], scalar1=-0.5)
+            nc.vector.tensor_scalar_mul(out=s["q_cap"][:], in0=s["q_gap"][:], scalar1=-2.0 / EPS)
+            nc.vector.tensor_scalar_mul(out=s["q_floor"][:], in0=s["q_gap"][:], scalar1=EPS / 2.0)
+
+        def spread_keys(h):
+            wide[h] = {}
+            for name in ("k_weight", "k_half"):
+                wide[h][name] = spread.tile([P, SEQ], F32, name=name)
+                for half in range(HALVES):
+                    bank = flip_banks.tile([P, BANK], F32, name="bank", tag="flip")
+                    for x in range(BANK // P):
+                        kt = half * (BANK // P) + x
+                        nc.tensor.transpose(
+                            bank[:, x * P : (x + 1) * P],
+                            small[h][name][:, kt : kt + 1].to_broadcast([P, P]),
+                            ident_f[:],
+                        )
+                    nc.vector.tensor_copy(out=wide[h][name][:, half * BANK : (half + 1) * BANK], in_=bank[:])
+
+        def scores(h, r):
+            s = small[h]
+            row = rows.tile([P, SEQ + 1], F32, name="row")
+            ratio[h, r] = row
+            for half in range(HALVES):
+                cols = slice(half * BANK, (half + 1) * BANK)
+                qk = score_banks.tile([P, BANK], F32, name="qk")
+                for c in range(CHUNKS):
+                    nc.tensor.matmul(
+                        out=qk[:],
+                        lhsT=q_flip[h][:, c, r * P : (r + 1) * P],
+                        rhs=k_flip[h][:, c, cols],
+                        start=(c == 0),
+                        stop=(c == CHUNKS - 1),
+                    )
+                nc.vector.scalar_tensor_tensor(
+                    out=row[:, cols], in0=qk[:], scalar=s["q_half"][:, r : r + 1], in1=wide[h]["k_half"][:, cols],
+                    op0=ALU.add, op1=ALU.subtract,
+                )
+            nc.vector.scalar_tensor_tensor(
+                out=row[:, :SEQ], in0=wide[h]["k_weight"][:], scalar=s["q_cap"][:, r : r + 1], in1=row[:, :SEQ],
+                op0=ALU.max, op1=ALU.mult,
+            )
+            nc.vector.tensor_scalar(
+                out=row[:, :SEQ], in0=row[:, :SEQ], scalar1=s["q_floor"][:, r : r + 1], scalar2=None,
+                op0=ALU.max, op1=ALU.min, accum_out=row[:, SEQ : SEQ + 1],
+            )
+
+        def multiply(h, r):
+            product[h, r] = work.tile([P, SEQ + 1], F32, name="product")
+            nc.vector.scalar_tensor_tensor(
+                out=product[h, r][:], in0=ratio[h, r][:], scalar=small[h]["q_gap"][:, r : r + 1], in1=ratio[h, r][:],
+                op0=ALU.add, op1=ALU.mult,
+            )
+
+        def root(h, r):
+            nc.scalar.activation(
+                out=product[h, r][:], in_=product[h, r][:], func=FUNC.Sqrt, scale=small[h]["q_inv2"][:, r : r + 1]
+            )
+
+        def add_root(h, r):
+            nc.vector.scalar_tensor_tensor(
+                out=ratio[h, r][:], in0=ratio[h, r][:], scalar=small[h]["q_inv"][:, r : r + 1], in1=product[h, r][:],
+                op0=ALU.mult, op1=ALU.add,
+            )
+
+        def log_and_square(h, r):
+            nc.scalar.activation(out=ratio[h, r][:], in_=ratio[h, r][:], func=FUNC.Ln, scale=2.0, bias=1.0)
+            nc.scalar.activation(out=ratio[h, r][:], in_=ratio[h, r][:], func=FUNC.Square)
+
+        def exponential(h, r):
+            e_bf[h, r] = work.tile([P, SEQ], BF16, name="e_bf")
+            nc.scalar.activation(
+                out=e_bf[h, r][:], in_=ratio[h, r][:, :SEQ], func=FUNC.Exp, scale=-1.0,
+                bias=ratio[h, r][:, SEQ : SEQ + 1], accum_out=small[h]["rowsum"][:, r : r + 1],
+            )
+            e_flip[h, r] = flip_banks.tile([P, TILES, P], BF16, name="e_flip", tag="flip")
+            for kt in range(TILES):
+                nc.tensor.transpose(e_flip[h, r][:, kt, :], e_bf[h, r][:, kt * P : (kt + 1) * P], ident_b[:])
+
+        def group(h, r):
+            e_grp[h, r] = work.tile([P, PASSES, P, PACK], BF16, name="e_grp", align_bytes=64)
+            nc.scalar.copy(out=e_grp[h, r][:], in_=e_flip[h, r][:].rearrange("p (g t) i -> p g i t", g=PASSES))
+
+        def quantise_and_multiply(h, r):
+            e_codes[h, r] = work.tile([P, PASSES * P], U32, name="e_codes", align_bytes=64)
+            e_scales[h, r] = work.tile([P, PASSES * P], U8, name="e_scales", align_bytes=64)
+            nc.vector.quantize_mx(
+                out=e_codes[h, r][:].bitcast(FP8X4),
+                scales=e_scales[h, r][:],
+                in_=e_grp[h, r][:].rearrange("p g i t -> p (g i t)"),
+            )
+            pv[h, r] = out_banks.tile([P, FEAT], F32, name="pv")
+            for g in range(PASSES):
+                nc.tensor.matmul_mx(
+                    out=pv[h, r][:],
+                    lhsT=e_codes[h, r][:, g * P : (g + 1) * P].bitcast(FP8X4),
+                    lhsT_scale=e_scales[h, r][:, g * P : (g + 1) * P],
+                    rhs=v_codes[h][:, g, :].bitcast(FP8X4),
+                    rhs_scale=v_scales[h][:, g, :],
+                    start=(g == 0),
+                    stop=(g == PASSES - 1),
+                )
+
+        def divide_and_store(h, r):
+            s = small[h]
+            nc.vector.reciprocal(out=s["rinv"][:, r : r + 1], in_=s["rowsum"][:, r : r + 1])
+            result = work.tile([P, FEAT], F32, name="result")
+            nc.vector.tensor_scalar_mul(out=result[:], in0=pv[h, r][:], scalar1=s["rinv"][:, r : r + 1])
+            nc.sync.dma_start(out=head_rows(out_rows, h).rearrange("(p r) d -> p r d", p=P)[:, r, :], in_=result[:])
+
+        def exp_step(h, step):
+            if step < TILES:
+                exponential(h, step)
+            if 0 <= step - 1 < TILES:
+                group(h, step - 1)
+            if 0 <= step - 2 < TILES:
+                quantise_and_multiply(h, step - 2)
+            if 0 <= step - 3 < TILES:
+                divide_and_store(h, step - 3)
+
+        load_qk(0)
+        load_qk(1)
+        load_v(0)
+        for step in range(TILES):
+            norms_and_flip(0, step, nc.vector.tensor_copy)
+        per_row_values(0)
+        spread_keys(0)
+        load_qk(2)
+        for r in range(TILES):
+            scores(0, r)
+            norms_and_flip(1, r, nc.scalar.copy)
+        per_row_values(1)
+        spread_keys(1)
+        quantise_v(0)
+
+        for h in range(HEADS):
+            if h + 3 < HEADS:
+                load_qk(h + 3)
+            if h + 1 < HEADS:
+                load_v(h + 1)
+
+            multiply(h, 0)
+            for r in range(TILES):
+                if r + 1 < TILES:
+                    multiply(h, r + 1)
+                root(h, r)
+                if h > 0 and r < CHAIN:
+                    exp_step(h - 1, TILES + r)
+                add_root(h, r)
+                if h + 2 < HEADS:
+                    norms_and_flip(h + 2, r, nc.scalar.copy)
+            if h + 2 < HEADS:
+                per_row_values(h + 2)
+                spread_keys(h + 2)
+            if h + 1 < HEADS:
+                quantise_v(h + 1)
+
+            for step in range(2 * TILES):
+                if h + 1 < HEADS and step % 2 == 0:
+                    scores(h + 1, step // 2)
+                if step < TILES:
+                    log_and_square(h, step)
+                else:
+                    exp_step(h, step - TILES)
+
+        for step in range(TILES, TILES + CHAIN):
+            exp_step(HEADS - 1, step)

@@ -19,11 +19,16 @@ TILES = SEQ // P
 CHUNKS = FEAT // P
 BANK = 512
 HALVES = SEQ // BANK
+BANKS = HALVES * TILES
 PACK = 4
 PASSES = SEQ // (P * PACK)
 EPS = 1e-7
 TINY = 1e-10
 CHAIN = 3
+AHEAD = 2
+LEAD = 2
+LAST = HEADS - 1
+assert BANKS == 2 * TILES
 FLOPS = 2 * 2 * HEADS * SEQ * SEQ * FEAT
 
 
@@ -42,6 +47,7 @@ def tile_riemannianattention_t_kernel(tc, query_states, key_states, value_states
         values = stack.enter_context(tc.tile_pool(name="values", bufs=1))
         rows = stack.enter_context(tc.tile_pool(name="rows", bufs=TILES + 6))
         work = stack.enter_context(tc.tile_pool(name="work", bufs=3))
+        products = stack.enter_context(tc.tile_pool(name="products", bufs=LEAD + 2))
         score_banks = stack.enter_context(tc.psum_pool(name="score_banks", bufs=4))
         flip_banks = stack.enter_context(tc.psum_pool(name="flip_banks", bufs=2))
         out_banks = stack.enter_context(tc.psum_pool(name="out_banks", bufs=2))
@@ -53,12 +59,13 @@ def tile_riemannianattention_t_kernel(tc, query_states, key_states, value_states
 
         stack.enter_context(tc.manual_schedule())
 
-        k_nat, q_nat, k_flip, q_flip, v_raw = {}, {}, {}, {}, {}
+        k_nat, q_nat, nat, k_flip, q_flip, v_raw = {}, {}, {}, {}, {}, {}
         v_codes, v_scales = {}, {}
         small = {}
         wide = {}
         ratio = {}
         product = {}
+        qk = {}
         e_bf, e_flip, e_grp, e_codes, e_scales, pv = {}, {}, {}, {}, {}, {}
 
         def head_rows(dram, h):
@@ -78,6 +85,7 @@ def tile_riemannianattention_t_kernel(tc, query_states, key_states, value_states
             small[h] = {}
             for name in ("kn", "qn", "rowsum"):
                 small[h][name] = keep.tile([P, TILES], F32, name="%s_%d" % (name, h))
+            nat[h] = {"kn": k_nat[h], "qn": q_nat[h]}
 
         def load_v(h):
             v_raw[h] = values.tile([P, PASSES, PACK, FEAT], BF16, name="v_raw")
@@ -98,28 +106,34 @@ def tile_riemannianattention_t_kernel(tc, query_states, key_states, value_states
                 in_=v_grp[:].rearrange("p g d t -> p (g d t)"),
             )
 
-        def norms_and_flip(h, step, copy_out):
+        def norm(h, step, name):
+            squares = work.tile([P, FEAT], BF16, name="squares")
+            nc.scalar.activation(
+                out=squares[:], in_=nat[h][name][:, step, :], func=FUNC.Square,
+                accum_out=small[h][name][:, step : step + 1],
+            )
+
+        def norm_on_vector(h, step, name):
+            squares_f = work.tile([P, FEAT], F32, name="squares_f")
+            nc.vector.scalar_tensor_tensor(
+                out=squares_f[:], in0=nat[h][name][:, step, :], scalar=1.0, in1=nat[h][name][:, step, :],
+                op0=ALU.mult, op1=ALU.mult, accum_out=small[h][name][:, step : step + 1],
+            )
+
+        def flip(h, step, copy_out):
             if step == 0:
                 k_flip[h] = flipped.tile([P, CHUNKS, SEQ], BF16, name="k_flip")
                 q_flip[h] = flipped.tile([P, CHUNKS, SEQ], BF16, name="q_flip")
-            for nat, name in ((k_nat[h], "kn"), (q_nat[h], "qn")):
-                squares = work.tile([P, FEAT], BF16, name="squares")
-                nc.scalar.activation(
-                    out=squares[:],
-                    in_=nat[:, step, :],
-                    func=FUNC.Square,
-                    accum_out=small[h][name][:, step : step + 1],
-                )
-            nat, flip = (k_nat[h], k_flip[h]) if step < CHUNKS else (q_nat[h], q_flip[h])
+            source, target = (k_nat[h], k_flip[h]) if step < CHUNKS else (q_nat[h], q_flip[h])
             c = step % CHUNKS
             bank = flip_banks.tile([P, SEQ], BF16, name="bank", tag="flip")
             for r in range(TILES):
-                nc.tensor.transpose(bank[:, r * P : (r + 1) * P], nat[:, r, c * P : (c + 1) * P], ident_b[:])
-            copy_out(out=flip[:, c, :], in_=bank[:])
+                nc.tensor.transpose(bank[:, r * P : (r + 1) * P], source[:, r, c * P : (c + 1) * P], ident_b[:])
+            copy_out(out=target[:, c, :], in_=bank[:])
 
         def per_row_values(h):
             s = small[h]
-            for name in ("k_gap", "k_weight", "k_half", "q_gap", "q_inv", "q_inv2", "q_half", "q_cap", "q_floor", "rinv"):
+            for name in ("k_gap", "k_weight", "k_half", "q_gap", "q_inv", "q_half", "q_cap", "q_floor", "rinv"):
                 s[name] = keep.tile([P, TILES], F32, name="%s_%d" % (name, h))
             for norm, gap in (("kn", "k_gap"), ("qn", "q_gap")):
                 nc.vector.tensor_scalar(out=s[gap][:], in0=s[norm][:], scalar1=-1.0, scalar2=1.0, op0=ALU.mult, op1=ALU.add)
@@ -128,7 +142,7 @@ def tile_riemannianattention_t_kernel(tc, query_states, key_states, value_states
             nc.vector.tensor_scalar_mul(out=s["k_weight"][:], in0=s["k_weight"][:], scalar1=-2.0)
             nc.vector.tensor_scalar_mul(out=s["k_half"][:], in0=s["kn"][:], scalar1=0.5)
             nc.vector.reciprocal(out=s["q_inv"][:], in_=s["q_gap"][:])
-            nc.vector.tensor_mul(out=s["q_inv2"][:], in0=s["q_inv"][:], in1=s["q_inv"][:])
+            nc.vector.tensor_scalar_mul(out=s["q_inv"][:], in0=s["q_inv"][:], scalar1=2.0)
             nc.vector.tensor_scalar_mul(out=s["q_half"][:], in0=s["qn"][:], scalar1=-0.5)
             nc.vector.tensor_scalar_mul(out=s["q_cap"][:], in0=s["q_gap"][:], scalar1=-2.0 / EPS)
             nc.vector.tensor_scalar_mul(out=s["q_floor"][:], in0=s["q_gap"][:], scalar1=EPS / 2.0)
@@ -148,55 +162,64 @@ def tile_riemannianattention_t_kernel(tc, query_states, key_states, value_states
                         )
                     nc.vector.tensor_copy(out=wide[h][name][:, half * BANK : (half + 1) * BANK], in_=bank[:])
 
-        def scores(h, r):
-            s = small[h]
-            row = rows.tile([P, SEQ + 1], F32, name="row")
-            ratio[h, r] = row
-            for half in range(HALVES):
-                cols = slice(half * BANK, (half + 1) * BANK)
-                qk = score_banks.tile([P, BANK], F32, name="qk")
-                for c in range(CHUNKS):
-                    nc.tensor.matmul(
-                        out=qk[:],
-                        lhsT=q_flip[h][:, c, r * P : (r + 1) * P],
-                        rhs=k_flip[h][:, c, cols],
-                        start=(c == 0),
-                        stop=(c == CHUNKS - 1),
-                    )
-                nc.vector.scalar_tensor_tensor(
-                    out=row[:, cols], in0=qk[:], scalar=s["q_half"][:, r : r + 1], in1=wide[h]["k_half"][:, cols],
-                    op0=ALU.add, op1=ALU.subtract,
+        def fill_bank(h, x):
+            r, half = divmod(x, HALVES)
+            qk[h, x] = score_banks.tile([P, BANK], F32, name="qk")
+            for c in range(CHUNKS):
+                nc.tensor.matmul(
+                    out=qk[h, x][:],
+                    lhsT=q_flip[h][:, c, r * P : (r + 1) * P],
+                    rhs=k_flip[h][:, c, half * BANK : (half + 1) * BANK],
+                    start=(c == 0),
+                    stop=(c == CHUNKS - 1),
                 )
+
+        def score_step(h, x):
+            s = small[h]
+            if x == 0:
+                for y in range(AHEAD):
+                    fill_bank(h, y)
+            if x + AHEAD < BANKS:
+                fill_bank(h, x + AHEAD)
+            r, half = divmod(x, HALVES)
+            if half == 0:
+                ratio[h, r] = rows.tile([P, SEQ + 1], F32, name="row")
+            row = ratio[h, r]
+            cols = slice(half * BANK, (half + 1) * BANK)
             nc.vector.scalar_tensor_tensor(
-                out=row[:, :SEQ], in0=wide[h]["k_weight"][:], scalar=s["q_cap"][:, r : r + 1], in1=row[:, :SEQ],
-                op0=ALU.max, op1=ALU.mult,
+                out=row[:, cols], in0=qk[h, x][:], scalar=s["q_half"][:, r : r + 1], in1=wide[h]["k_half"][:, cols],
+                op0=ALU.add, op1=ALU.subtract,
             )
-            nc.vector.tensor_scalar(
-                out=row[:, :SEQ], in0=row[:, :SEQ], scalar1=s["q_floor"][:, r : r + 1], scalar2=None,
-                op0=ALU.max, op1=ALU.min, accum_out=row[:, SEQ : SEQ + 1],
-            )
+            if half == HALVES - 1:
+                nc.vector.scalar_tensor_tensor(
+                    out=row[:, :SEQ], in0=wide[h]["k_weight"][:], scalar=s["q_cap"][:, r : r + 1], in1=row[:, :SEQ],
+                    op0=ALU.max, op1=ALU.mult,
+                )
+                nc.vector.tensor_scalar(
+                    out=row[:, :SEQ], in0=row[:, :SEQ], scalar1=s["q_floor"][:, r : r + 1], scalar2=None,
+                    op0=ALU.max, op1=ALU.min, accum_out=row[:, SEQ : SEQ + 1],
+                )
 
         def multiply(h, r):
-            product[h, r] = work.tile([P, SEQ + 1], F32, name="product")
+            product[h, r] = products.tile([P, SEQ + 1], F32, name="product")
             nc.vector.scalar_tensor_tensor(
                 out=product[h, r][:], in0=ratio[h, r][:], scalar=small[h]["q_gap"][:, r : r + 1], in1=ratio[h, r][:],
                 op0=ALU.add, op1=ALU.mult,
             )
 
         def root(h, r):
-            nc.scalar.activation(
-                out=product[h, r][:], in_=product[h, r][:], func=FUNC.Sqrt, scale=small[h]["q_inv2"][:, r : r + 1]
-            )
+            nc.scalar.activation(out=product[h, r][:], in_=product[h, r][:], func=FUNC.Sqrt)
 
         def add_root(h, r):
-            nc.vector.scalar_tensor_tensor(
-                out=ratio[h, r][:], in0=ratio[h, r][:], scalar=small[h]["q_inv"][:, r : r + 1], in1=product[h, r][:],
-                op0=ALU.mult, op1=ALU.add,
-            )
+            nc.vector.tensor_add(out=ratio[h, r][:], in0=ratio[h, r][:], in1=product[h, r][:])
 
         def log_and_square(h, r):
-            nc.scalar.activation(out=ratio[h, r][:], in_=ratio[h, r][:], func=FUNC.Ln, scale=2.0, bias=1.0)
-            nc.scalar.activation(out=ratio[h, r][:], in_=ratio[h, r][:], func=FUNC.Square)
+            row = ratio[h, r]
+            nc.scalar.activation(out=row[:], in_=row[:], func=FUNC.Ln, scale=small[h]["q_inv"][:, r : r + 1], bias=1.0)
+            if h == LAST:
+                nc.vector.tensor_mul(out=row[:], in0=row[:], in1=row[:])
+            else:
+                nc.scalar.activation(out=row[:], in_=row[:], func=FUNC.Square)
 
         def exponential(h, r):
             e_bf[h, r] = work.tile([P, SEQ], BF16, name="e_bf")
@@ -210,7 +233,8 @@ def tile_riemannianattention_t_kernel(tc, query_states, key_states, value_states
 
         def group(h, r):
             e_grp[h, r] = work.tile([P, PASSES, P, PACK], BF16, name="e_grp", align_bytes=64)
-            nc.scalar.copy(out=e_grp[h, r][:], in_=e_flip[h, r][:].rearrange("p (g t) i -> p g i t", g=PASSES))
+            copy_out = nc.vector.tensor_copy if h == LAST else nc.scalar.copy
+            copy_out(out=e_grp[h, r][:], in_=e_flip[h, r][:].rearrange("p (g t) i -> p g i t", g=PASSES))
 
         def quantise_and_multiply(h, r):
             e_codes[h, r] = work.tile([P, PASSES * P], U32, name="e_codes", align_bytes=64)
@@ -253,46 +277,57 @@ def tile_riemannianattention_t_kernel(tc, query_states, key_states, value_states
         load_qk(1)
         load_v(0)
         for step in range(TILES):
-            norms_and_flip(0, step, nc.vector.tensor_copy)
+            norm(0, step, "kn")
+            norm_on_vector(0, step, "qn")
+            flip(0, step, nc.vector.tensor_copy)
         per_row_values(0)
         spread_keys(0)
         load_qk(2)
-        for r in range(TILES):
-            scores(0, r)
-            norms_and_flip(1, r, nc.scalar.copy)
+        for x in range(BANKS):
+            score_step(0, x)
+            if x < TILES:
+                flip(1, x, nc.scalar.copy)
+                norm(1, x, "kn")
+                norm(1, x, "qn")
+            else:
+                norm(2, x - TILES, "kn")
+                norm(2, x - TILES, "qn")
+            if x == TILES - 1:
+                load_qk(3)
+        for r in range(LEAD):
+            multiply(0, r)
         per_row_values(1)
         spread_keys(1)
-        quantise_v(0)
 
         for h in range(HEADS):
-            if h + 3 < HEADS:
-                load_qk(h + 3)
-            if h + 1 < HEADS:
-                load_v(h + 1)
-
-            multiply(h, 0)
             for r in range(TILES):
-                if r + 1 < TILES:
-                    multiply(h, r + 1)
+                if r + LEAD < TILES:
+                    multiply(h, r + LEAD)
                 root(h, r)
                 if h > 0 and r < CHAIN:
                     exp_step(h - 1, TILES + r)
                 add_root(h, r)
                 if h + 2 < HEADS:
-                    norms_and_flip(h + 2, r, nc.scalar.copy)
+                    flip(h + 2, r, nc.scalar.copy)
+                if h + 3 < HEADS:
+                    norm(h + 3, r, "kn")
+                    norm(h + 3, r, "qn")
+            quantise_v(h)
+            if h + 1 < HEADS:
+                load_v(h + 1)
             if h + 2 < HEADS:
                 per_row_values(h + 2)
                 spread_keys(h + 2)
-            if h + 1 < HEADS:
-                quantise_v(h + 1)
 
-            for step in range(2 * TILES):
-                if h + 1 < HEADS and step % 2 == 0:
-                    scores(h + 1, step // 2)
+            for step in range(BANKS):
+                if h + 1 < HEADS:
+                    score_step(h + 1, step)
                 if step < TILES:
                     log_and_square(h, step)
                 else:
                     exp_step(h, step - TILES)
+                if h + 1 < HEADS and step >= BANKS - LEAD:
+                    multiply(h + 1, step - (BANKS - LEAD))
 
         for step in range(TILES, TILES + CHAIN):
-            exp_step(HEADS - 1, step)
+            exp_step(LAST, step)

@@ -60,7 +60,7 @@ def tile_riemannianattention_t_kernel(tc, query_states, key_states, value_states
         stack.enter_context(tc.manual_schedule())
 
         k_nat, q_nat, nat, k_flip, q_flip, v_raw = {}, {}, {}, {}, {}, {}
-        v_codes, v_scales = {}, {}
+        v_grp, v_codes, v_scales = {}, {}, {}
         small = {}
         wide = {}
         ratio = {}
@@ -94,16 +94,18 @@ def tile_riemannianattention_t_kernel(tc, query_states, key_states, value_states
                 in_=head_rows(v_rows, h).rearrange("(g p t) d -> p g (t d)", g=PASSES, p=P),
             )
 
-        def quantise_v(h):
-            v_grp = values.tile([P, PASSES, FEAT, PACK], BF16, name="v_grp", align_bytes=64)
+        def group_v(h):
+            v_grp[h] = values.tile([P, PASSES, FEAT, PACK], BF16, name="v_grp", align_bytes=64)
             for g in range(PASSES):
-                nc.vector.tensor_copy(out=v_grp[:, g], in_=v_raw[h][:, g].rearrange("p t d -> p d t"))
+                nc.vector.tensor_copy(out=v_grp[h][:, g], in_=v_raw[h][:, g].rearrange("p t d -> p d t"))
+
+        def quantise_v(h):
             v_codes[h] = keep.tile([P, PASSES, FEAT], U32, name="v_codes_%d" % h, align_bytes=64)
             v_scales[h] = keep.tile([P, PASSES, FEAT], U8, name="v_scales_%d" % h, align_bytes=64)
             nc.vector.quantize_mx(
                 out=v_codes[h][:].rearrange("p g d -> p (g d)").bitcast(FP8X4),
                 scales=v_scales[h][:].rearrange("p g d -> p (g d)"),
-                in_=v_grp[:].rearrange("p g d t -> p (g d t)"),
+                in_=v_grp[h][:].rearrange("p g d t -> p (g d t)"),
             )
 
         def norm(h, step, name):
@@ -111,13 +113,6 @@ def tile_riemannianattention_t_kernel(tc, query_states, key_states, value_states
             nc.scalar.activation(
                 out=squares[:], in_=nat[h][name][:, step, :], func=FUNC.Square,
                 accum_out=small[h][name][:, step : step + 1],
-            )
-
-        def norm_on_vector(h, step, name):
-            squares_f = work.tile([P, FEAT], F32, name="squares_f")
-            nc.vector.scalar_tensor_tensor(
-                out=squares_f[:], in0=nat[h][name][:, step, :], scalar=1.0, in1=nat[h][name][:, step, :],
-                op0=ALU.mult, op1=ALU.mult, accum_out=small[h][name][:, step : step + 1],
             )
 
         def flip(h, step, copy_out):
@@ -131,21 +126,33 @@ def tile_riemannianattention_t_kernel(tc, query_states, key_states, value_states
                 nc.tensor.transpose(bank[:, r * P : (r + 1) * P], source[:, r, c * P : (c + 1) * P], ident_b[:])
             copy_out(out=target[:, c, :], in_=bank[:])
 
-        def per_row_values(h):
+        def gap_to_the_rim(h, norm_name, gap_name):
             s = small[h]
-            for name in ("k_gap", "k_weight", "k_half", "q_gap", "q_inv", "q_half", "q_cap", "q_floor", "rinv"):
+            s[gap_name] = keep.tile([P, TILES], F32, name="%s_%d" % (gap_name, h))
+            nc.vector.tensor_scalar(
+                out=s[gap_name][:], in0=s[norm_name][:], scalar1=-1.0, scalar2=1.0, op0=ALU.mult, op1=ALU.add
+            )
+            nc.vector.tensor_scalar_max(out=s[gap_name][:], in0=s[gap_name][:], scalar1=TINY)
+
+        def key_values(h):
+            s = small[h]
+            gap_to_the_rim(h, "kn", "k_gap")
+            for name in ("k_weight", "k_half"):
                 s[name] = keep.tile([P, TILES], F32, name="%s_%d" % (name, h))
-            for norm, gap in (("kn", "k_gap"), ("qn", "q_gap")):
-                nc.vector.tensor_scalar(out=s[gap][:], in0=s[norm][:], scalar1=-1.0, scalar2=1.0, op0=ALU.mult, op1=ALU.add)
-                nc.vector.tensor_scalar_max(out=s[gap][:], in0=s[gap][:], scalar1=TINY)
             nc.vector.reciprocal(out=s["k_weight"][:], in_=s["k_gap"][:])
-            nc.vector.tensor_scalar_mul(out=s["k_weight"][:], in0=s["k_weight"][:], scalar1=-2.0)
             nc.vector.tensor_scalar_mul(out=s["k_half"][:], in0=s["kn"][:], scalar1=0.5)
+            nc.vector.tensor_scalar_mul(out=s["k_weight"][:], in0=s["k_weight"][:], scalar1=-2.0)
+
+        def query_values(h):
+            s = small[h]
+            gap_to_the_rim(h, "qn", "q_gap")
+            for name in ("q_inv", "q_half", "q_cap", "q_floor", "rinv"):
+                s[name] = keep.tile([P, TILES], F32, name="%s_%d" % (name, h))
             nc.vector.reciprocal(out=s["q_inv"][:], in_=s["q_gap"][:])
-            nc.vector.tensor_scalar_mul(out=s["q_inv"][:], in0=s["q_inv"][:], scalar1=2.0)
             nc.vector.tensor_scalar_mul(out=s["q_half"][:], in0=s["qn"][:], scalar1=-0.5)
             nc.vector.tensor_scalar_mul(out=s["q_cap"][:], in0=s["q_gap"][:], scalar1=-2.0 / EPS)
             nc.vector.tensor_scalar_mul(out=s["q_floor"][:], in0=s["q_gap"][:], scalar1=EPS / 2.0)
+            nc.vector.tensor_scalar_mul(out=s["q_inv"][:], in0=s["q_inv"][:], scalar1=2.0)
 
         def spread_keys(h):
             wide[h] = {}
@@ -181,20 +188,25 @@ def tile_riemannianattention_t_kernel(tc, query_states, key_states, value_states
                     fill_bank(h, y)
             if x + AHEAD < BANKS:
                 fill_bank(h, x + AHEAD)
-            r, half = divmod(x, HALVES)
-            if half == 0:
-                ratio[h, r] = rows.tile([P, SEQ + 1], F32, name="row")
-            row = ratio[h, r]
-            cols = slice(half * BANK, (half + 1) * BANK)
-            nc.vector.scalar_tensor_tensor(
-                out=row[:, cols], in0=qk[h, x][:], scalar=s["q_half"][:, r : r + 1], in1=wide[h]["k_half"][:, cols],
-                op0=ALU.add, op1=ALU.subtract,
-            )
-            if half == HALVES - 1:
+            if x < BANKS:
+                r, half = divmod(x, HALVES)
+                if half == 0:
+                    ratio[h, r] = rows.tile([P, SEQ + 1], F32, name="row")
+                cols = slice(half * BANK, (half + 1) * BANK)
+                nc.vector.scalar_tensor_tensor(
+                    out=ratio[h, r][:, cols], in0=qk[h, x][:], scalar=s["q_half"][:, r : r + 1],
+                    in1=wide[h]["k_half"][:, cols], op0=ALU.add, op1=ALU.subtract,
+                )
+            if x >= HALVES and x % HALVES == 0:
+                r = x // HALVES - 1
+                row = ratio[h, r]
                 nc.vector.scalar_tensor_tensor(
                     out=row[:, :SEQ], in0=wide[h]["k_weight"][:], scalar=s["q_cap"][:, r : r + 1], in1=row[:, :SEQ],
                     op0=ALU.max, op1=ALU.mult,
                 )
+            if x > HALVES and x % HALVES == 1:
+                r = x // HALVES - 1
+                row = ratio[h, r]
                 nc.vector.tensor_scalar(
                     out=row[:, :SEQ], in0=row[:, :SEQ], scalar1=s["q_floor"][:, r : r + 1], scalar2=None,
                     op0=ALU.max, op1=ALU.min, accum_out=row[:, SEQ : SEQ + 1],
@@ -213,9 +225,12 @@ def tile_riemannianattention_t_kernel(tc, query_states, key_states, value_states
         def add_root(h, r):
             nc.vector.tensor_add(out=ratio[h, r][:], in0=ratio[h, r][:], in1=product[h, r][:])
 
-        def log_and_square(h, r):
+        def logarithm(h, r):
             row = ratio[h, r]
             nc.scalar.activation(out=row[:], in_=row[:], func=FUNC.Ln, scale=small[h]["q_inv"][:, r : r + 1], bias=1.0)
+
+        def square(h, r):
+            row = ratio[h, r]
             if h == LAST:
                 nc.vector.tensor_mul(out=row[:], in0=row[:], in1=row[:])
             else:
@@ -244,6 +259,7 @@ def tile_riemannianattention_t_kernel(tc, query_states, key_states, value_states
                 scales=e_scales[h, r][:],
                 in_=e_grp[h, r][:].rearrange("p g i t -> p (g i t)"),
             )
+            nc.vector.reciprocal(out=small[h]["rinv"][:, r : r + 1], in_=small[h]["rowsum"][:, r : r + 1])
             pv[h, r] = out_banks.tile([P, FEAT], F32, name="pv")
             for g in range(PASSES):
                 nc.tensor.matmul_mx(
@@ -257,10 +273,8 @@ def tile_riemannianattention_t_kernel(tc, query_states, key_states, value_states
                 )
 
         def divide_and_store(h, r):
-            s = small[h]
-            nc.vector.reciprocal(out=s["rinv"][:, r : r + 1], in_=s["rowsum"][:, r : r + 1])
             result = work.tile([P, FEAT], F32, name="result")
-            nc.vector.tensor_scalar_mul(out=result[:], in0=pv[h, r][:], scalar1=s["rinv"][:, r : r + 1])
+            nc.vector.tensor_scalar_mul(out=result[:], in0=pv[h, r][:], scalar1=small[h]["rinv"][:, r : r + 1])
             nc.sync.dma_start(out=head_rows(out_rows, h).rearrange("(p r) d -> p r d", p=P)[:, r, :], in_=result[:])
 
         def exp_step(h, step):
@@ -278,29 +292,34 @@ def tile_riemannianattention_t_kernel(tc, query_states, key_states, value_states
         load_v(0)
         for step in range(TILES):
             norm(0, step, "kn")
-            norm_on_vector(0, step, "qn")
             flip(0, step, nc.vector.tensor_copy)
-        per_row_values(0)
+        key_values(0)
         spread_keys(0)
+        for step in range(TILES):
+            norm(0, step, "qn")
+        query_values(0)
         load_qk(2)
-        for x in range(BANKS):
+        for x in range(BANKS + 2):
             score_step(0, x)
             if x < TILES:
                 flip(1, x, nc.scalar.copy)
                 norm(1, x, "kn")
                 norm(1, x, "qn")
-            else:
+            elif x < BANKS:
                 norm(2, x - TILES, "kn")
                 norm(2, x - TILES, "qn")
             if x == TILES - 1:
                 load_qk(3)
         for r in range(LEAD):
             multiply(0, r)
-        per_row_values(1)
+        key_values(1)
+        query_values(1)
         spread_keys(1)
 
         for h in range(HEADS):
             for r in range(TILES):
+                if h > 0 and r < 2:
+                    score_step(h, BANKS + r)
                 if r + LEAD < TILES:
                     multiply(h, r + LEAD)
                 root(h, r)
@@ -312,19 +331,23 @@ def tile_riemannianattention_t_kernel(tc, query_states, key_states, value_states
                 if h + 3 < HEADS:
                     norm(h + 3, r, "kn")
                     norm(h + 3, r, "qn")
+            group_v(h)
+            if h + 2 < HEADS:
+                key_values(h + 2)
+                query_values(h + 2)
+                spread_keys(h + 2)
             quantise_v(h)
             if h + 1 < HEADS:
                 load_v(h + 1)
-            if h + 2 < HEADS:
-                per_row_values(h + 2)
-                spread_keys(h + 2)
 
             for step in range(BANKS):
                 if h + 1 < HEADS:
                     score_step(h + 1, step)
                 if step < TILES:
-                    log_and_square(h, step)
-                else:
+                    logarithm(h, step)
+                if 1 <= step <= TILES:
+                    square(h, step - 1)
+                if step >= TILES:
                     exp_step(h, step - TILES)
                 if h + 1 < HEADS and step >= BANKS - LEAD:
                     multiply(h + 1, step - (BANKS - LEAD))

@@ -41,9 +41,9 @@ def tile_riemannianattention_t_kernel(tc, query_states, key_states, value_states
 
     with ExitStack() as stack:
         keep = stack.enter_context(tc.tile_pool(name="keep", bufs=1))
-        natural = stack.enter_context(tc.tile_pool(name="natural", bufs=2))
+        natural = stack.enter_context(tc.tile_pool(name="natural", bufs=3))
         flipped = stack.enter_context(tc.tile_pool(name="flipped", bufs=2))
-        spread = stack.enter_context(tc.tile_pool(name="spread", bufs=2))
+        spread = stack.enter_context(tc.tile_pool(name="spread", bufs=1))
         values = stack.enter_context(tc.tile_pool(name="values", bufs=1))
         rows = stack.enter_context(tc.tile_pool(name="rows", bufs=TILES + 6))
         work = stack.enter_context(tc.tile_pool(name="work", bufs=3))
@@ -274,7 +274,7 @@ def tile_riemannianattention_t_kernel(tc, query_states, key_states, value_states
 
         def divide_and_store(h, r):
             result = work.tile([P, FEAT], F32, name="result")
-            nc.vector.tensor_scalar_mul(out=result[:], in0=pv[h, r][:], scalar1=small[h]["rinv"][:, r : r + 1])
+            nc.scalar.activation(out=result[:], in_=pv[h, r][:], func=FUNC.Copy, scale=small[h]["rinv"][:, r : r + 1])
             nc.sync.dma_start(out=head_rows(out_rows, h).rearrange("(p r) d -> p r d", p=P)[:, r, :], in_=result[:])
 
         def exp_step(h, step):
@@ -289,6 +289,7 @@ def tile_riemannianattention_t_kernel(tc, query_states, key_states, value_states
 
         load_qk(0)
         load_qk(1)
+        load_qk(2)
         load_v(0)
         for step in range(TILES):
             norm(0, step, "kn")
@@ -298,23 +299,19 @@ def tile_riemannianattention_t_kernel(tc, query_states, key_states, value_states
         for step in range(TILES):
             norm(0, step, "qn")
         query_values(0)
-        load_qk(2)
+        load_qk(3)
+        for step in range(TILES):
+            norm(1, step, "kn")
+            norm(1, step, "qn")
         for x in range(BANKS + 2):
             score_step(0, x)
             if x < TILES:
                 flip(1, x, nc.scalar.copy)
-                norm(1, x, "kn")
-                norm(1, x, "qn")
-            elif x < BANKS:
-                norm(2, x - TILES, "kn")
-                norm(2, x - TILES, "qn")
-            if x == TILES - 1:
-                load_qk(3)
+            if x < BANKS:
+                norm(2 + x // TILES, x % TILES, "kn")
+                norm(2 + x // TILES, x % TILES, "qn")
         for r in range(LEAD):
             multiply(0, r)
-        key_values(1)
-        query_values(1)
-        spread_keys(1)
 
         for h in range(HEADS):
             for r in range(TILES):
@@ -328,14 +325,13 @@ def tile_riemannianattention_t_kernel(tc, query_states, key_states, value_states
                 add_root(h, r)
                 if h + 2 < HEADS:
                     flip(h + 2, r, nc.scalar.copy)
-                if h + 3 < HEADS:
-                    norm(h + 3, r, "kn")
-                    norm(h + 3, r, "qn")
+
+            if h + 1 < HEADS:
+                key_values(h + 1)
             group_v(h)
-            if h + 2 < HEADS:
-                key_values(h + 2)
-                query_values(h + 2)
-                spread_keys(h + 2)
+            if h + 1 < HEADS:
+                query_values(h + 1)
+                spread_keys(h + 1)
             quantise_v(h)
             if h + 1 < HEADS:
                 load_v(h + 1)

@@ -26,7 +26,7 @@ EPS = 1e-7
 TINY = 1e-10
 CHAIN = 3
 AHEAD = 2
-LEAD = 2
+LEAD = 5
 LAST = HEADS - 1
 assert BANKS == 2 * TILES
 FLOPS = 2 * 2 * HEADS * SEQ * SEQ * FEAT
@@ -45,7 +45,7 @@ def tile_riemannianattention_t_kernel(tc, query_states, key_states, value_states
         flipped = stack.enter_context(tc.tile_pool(name="flipped", bufs=2))
         spread = stack.enter_context(tc.tile_pool(name="spread", bufs=1))
         values = stack.enter_context(tc.tile_pool(name="values", bufs=1))
-        rows = stack.enter_context(tc.tile_pool(name="rows", bufs=TILES + 6))
+        rows = stack.enter_context(tc.tile_pool(name="rows", bufs=TILES + 5))
         work = stack.enter_context(tc.tile_pool(name="work", bufs=3))
         products = stack.enter_context(tc.tile_pool(name="products", bufs=LEAD + 2))
         score_banks = stack.enter_context(tc.psum_pool(name="score_banks", bufs=4))

from contextlib import ExitStack

import concourse.mybir as mybir
from concourse.masks import make_identity

F32 = mybir.dt.float32
BF16 = mybir.dt.bfloat16
U32 = mybir.dt.uint32
U8 = mybir.dt.uint8
FP8X4 = mybir.dt.float8_e4m3fn_x4
ALU = mybir.AluOpType
FUNC = mybir.ActivationFunctionType

P = 128
HEADS = 4
SEQ = 1024
FEAT = 512
TILES = SEQ // P
CHUNKS = FEAT // P
BANK = 512
HALVES = SEQ // BANK
BANKS = HALVES * TILES
PACK = 4
PASSES = SEQ // (P * PACK)
EPS = 1e-7
TINY = 1e-10
CHAIN = 3
AHEAD = 2
LEAD = 5
LAST = HEADS - 1
assert BANKS == 2 * TILES
FLOPS = 2 * 2 * HEADS * SEQ * SEQ * FEAT


def tile_riemannianattention_t_kernel(tc, query_states, key_states, value_states, out):
    nc = tc.nc
    q_rows = query_states.flatten_outer_dims()
    k_rows = key_states.flatten_outer_dims()
    v_rows = value_states.flatten_outer_dims()
    out_rows = out.flatten_outer_dims()

    with ExitStack() as stack:
        keep = stack.enter_context(tc.tile_pool(name="keep", bufs=1))
        natural = stack.enter_context(tc.tile_pool(name="natural", bufs=3))
        flipped = stack.enter_context(tc.tile_pool(name="flipped", bufs=2))
        spread = stack.enter_context(tc.tile_pool(name="spread", bufs=1))
        values = stack.enter_context(tc.tile_pool(name="values", bufs=1))
        rows = stack.enter_context(tc.tile_pool(name="rows", bufs=TILES + 5))
        work = stack.enter_context(tc.tile_pool(name="work", bufs=3))
        products = stack.enter_context(tc.tile_pool(name="products", bufs=LEAD + 2))
        score_banks = stack.enter_context(tc.psum_pool(name="score_banks", bufs=4))
        flip_banks = stack.enter_context(tc.psum_pool(name="flip_banks", bufs=2))
        out_banks = stack.enter_context(tc.psum_pool(name="out_banks", bufs=2))

        ident_b = keep.tile([P, P], BF16, name="ident_b")
        make_identity(nc, ident_b[:])
        ident_f = keep.tile([P, P], F32, name="ident_f")
        make_identity(nc, ident_f[:])

        stack.enter_context(tc.manual_schedule())

        k_nat, q_nat, nat, k_flip, q_flip, v_raw = {}, {}, {}, {}, {}, {}
        v_grp, v_codes, v_scales = {}, {}, {}
        small = {}
        wide = {}
        ratio = {}
        product = {}
        qk = {}
        e_bf, e_flip, e_grp, e_codes, e_scales, pv = {}, {}, {}, {}, {}, {}

        def head_rows(dram, h):
            return dram[h * SEQ : (h + 1) * SEQ, :]

        def load_qk(h):
            k_nat[h] = natural.tile([P, TILES, FEAT], BF16, name="k_nat")
            nc.sync.dma_start(
                out=k_nat[h][:].rearrange("p (g t) d -> p g (t d)", g=PASSES),
                in_=head_rows(k_rows, h).rearrange("(g p t) d -> p g (t d)", g=PASSES, p=P),
            )
            q_nat[h] = natural.tile([P, TILES, FEAT], BF16, name="q_nat")
            nc.sync.dma_start(
                out=q_nat[h][:].rearrange("p r d -> p (r d)"),
                in_=head_rows(q_rows, h).rearrange("(p r) d -> p (r d)", p=P),
            )
            small[h] = {}
            for name in ("kn", "qn", "rowsum"):
                small[h][name] = keep.tile([P, TILES], F32, name="%s_%d" % (name, h))
            nat[h] = {"kn": k_nat[h], "qn": q_nat[h]}

        def load_v(h):
            v_raw[h] = values.tile([P, PASSES, PACK, FEAT], BF16, name="v_raw")
            nc.sync.dma_start(
                out=v_raw[h][:].rearrange("p g t d -> p g (t d)"),
                in_=head_rows(v_rows, h).rearrange("(g p t) d -> p g (t d)", g=PASSES, p=P),
            )

        def group_v(h):
            v_grp[h] = values.tile([P, PASSES, FEAT, PACK], BF16, name="v_grp", align_bytes=64)
            for g in range(PASSES):
                nc.vector.tensor_copy(out=v_grp[h][:, g], in_=v_raw[h][:, g].rearrange("p t d -> p d t"))

        def quantise_v(h):
            v_codes[h] = keep.tile([P, PASSES, FEAT], U32, name="v_codes_%d" % h, align_bytes=64)
            v_scales[h] = keep.tile([P, PASSES, FEAT], U8, name="v_scales_%d" % h, align_bytes=64)
            nc.vector.quantize_mx(
                out=v_codes[h][:].rearrange("p g d -> p (g d)").bitcast(FP8X4),
                scales=v_scales[h][:].rearrange("p g d -> p (g d)"),
                in_=v_grp[h][:].rearrange("p g d t -> p (g d t)"),
            )

        def norm(h, step, name):
            squares = work.tile([P, FEAT], BF16, name="squares")
            nc.scalar.activation(
                out=squares[:], in_=nat[h][name][:, step, :], func=FUNC.Square,
                accum_out=small[h][name][:, step : step + 1],
            )

        def flip(h, step, copy_out):
            if step == 0:
                k_flip[h] = flipped.tile([P, CHUNKS, SEQ], BF16, name="k_flip")
                q_flip[h] = flipped.tile([P, CHUNKS, SEQ], BF16, name="q_flip")
            source, target = (k_nat[h], k_flip[h]) if step < CHUNKS else (q_nat[h], q_flip[h])
            c = step % CHUNKS
            bank = flip_banks.tile([P, SEQ], BF16, name="bank", tag="flip")
            for r in range(TILES):
                nc.tensor.transpose(bank[:, r * P : (r + 1) * P], source[:, r, c * P : (c + 1) * P], ident_b[:])
            copy_out(out=target[:, c, :], in_=bank[:])

        def gap_to_the_rim(h, norm_name, gap_name):
            s = small[h]
            s[gap_name] = keep.tile([P, TILES], F32, name="%s_%d" % (gap_name, h))
            nc.vector.tensor_scalar(
                out=s[gap_name][:], in0=s[norm_name][:], scalar1=-1.0, scalar2=1.0, op0=ALU.mult, op1=ALU.add
            )
            nc.vector.tensor_scalar_max(out=s[gap_name][:], in0=s[gap_name][:], scalar1=TINY)

        def key_values(h):
            s = small[h]
            gap_to_the_rim(h, "kn", "k_gap")
            for name in ("k_weight", "k_half"):
                s[name] = keep.tile([P, TILES], F32, name="%s_%d" % (name, h))
            nc.vector.reciprocal(out=s["k_weight"][:], in_=s["k_gap"][:])
            nc.vector.tensor_scalar_mul(out=s["k_half"][:], in0=s["kn"][:], scalar1=0.5)
            nc.vector.tensor_scalar_mul(out=s["k_weight"][:], in0=s["k_weight"][:], scalar1=-2.0)

        def query_values(h):
            s = small[h]
            gap_to_the_rim(h, "qn", "q_gap")
            for name in ("q_inv", "q_half", "q_cap", "q_floor", "rinv"):
                s[name] = keep.tile([P, TILES], F32, name="%s_%d" % (name, h))
            nc.vector.reciprocal(out=s["q_inv"][:], in_=s["q_gap"][:])
            nc.vector.tensor_scalar_mul(out=s["q_half"][:], in0=s["qn"][:], scalar1=-0.5)
            nc.vector.tensor_scalar_mul(out=s["q_cap"][:], in0=s["q_gap"][:], scalar1=-2.0 / EPS)
            nc.vector.tensor_scalar_mul(out=s["q_floor"][:], in0=s["q_gap"][:], scalar1=EPS / 2.0)
            nc.vector.tensor_scalar_mul(out=s["q_inv"][:], in0=s["q_inv"][:], scalar1=2.0)

        def spread_keys(h):
            wide[h] = {}
            for name in ("k_weight", "k_half"):
                wide[h][name] = spread.tile([P, SEQ], F32, name=name)
                for half in range(HALVES):
                    bank = flip_banks.tile([P, BANK], F32, name="bank", tag="flip")
                    for x in range(BANK // P):
                        kt = half * (BANK // P) + x
                        nc.tensor.transpose(
                            bank[:, x * P : (x + 1) * P],
                            small[h][name][:, kt : kt + 1].to_broadcast([P, P]),
                            ident_f[:],
                        )
                    nc.vector.tensor_copy(out=wide[h][name][:, half * BANK : (half + 1) * BANK], in_=bank[:])

        def fill_bank(h, x):
            r, half = divmod(x, HALVES)
            qk[h, x] = score_banks.tile([P, BANK], F32, name="qk")
            for c in range(CHUNKS):
                nc.tensor.matmul(
                    out=qk[h, x][:],
                    lhsT=q_flip[h][:, c, r * P : (r + 1) * P],
                    rhs=k_flip[h][:, c, half * BANK : (half + 1) * BANK],
                    start=(c == 0),
                    stop=(c == CHUNKS - 1),
                )

        def score_step(h, x):
            s = small[h]
            if x == 0:
                for y in range(AHEAD):
                    fill_bank(h, y)
            if x + AHEAD < BANKS:
                fill_bank(h, x + AHEAD)
            if x < BANKS:
                r, half = divmod(x, HALVES)
                if half == 0:
                    ratio[h, r] = rows.tile([P, SEQ + 1], F32, name="row")
                cols = slice(half * BANK, (half + 1) * BANK)
                nc.vector.scalar_tensor_tensor(
                    out=ratio[h, r][:, cols], in0=qk[h, x][:], scalar=s["q_half"][:, r : r + 1],
                    in1=wide[h]["k_half"][:, cols], op0=ALU.add, op1=ALU.subtract,
                )
            if x >= HALVES and x % HALVES == 0:
                r = x // HALVES - 1
                row = ratio[h, r]
                nc.vector.scalar_tensor_tensor(
                    out=row[:, :SEQ], in0=wide[h]["k_weight"][:], scalar=s["q_cap"][:, r : r + 1], in1=row[:, :SEQ],
                    op0=ALU.max, op1=ALU.mult,
                )
            if x > HALVES and x % HALVES == 1:
                r = x // HALVES - 1
                row = ratio[h, r]
                nc.vector.tensor_scalar(
                    out=row[:, :SEQ], in0=row[:, :SEQ], scalar1=s["q_floor"][:, r : r + 1], scalar2=None,
                    op0=ALU.max, op1=ALU.min, accum_out=row[:, SEQ : SEQ + 1],
                )

        def multiply(h, r):
            product[h, r] = products.tile([P, SEQ + 1], F32, name="product")
            nc.vector.scalar_tensor_tensor(
                out=product[h, r][:], in0=ratio[h, r][:], scalar=small[h]["q_gap"][:, r : r + 1], in1=ratio[h, r][:],
                op0=ALU.add, op1=ALU.mult,
            )

        def root(h, r):
            nc.scalar.activation(out=product[h, r][:], in_=product[h, r][:], func=FUNC.Sqrt)

        def add_root(h, r):
            nc.vector.tensor_add(out=ratio[h, r][:], in0=ratio[h, r][:], in1=product[h, r][:])

        def logarithm(h, r):
            row = ratio[h, r]
            nc.scalar.activation(out=row[:], in_=row[:], func=FUNC.Ln, scale=small[h]["q_inv"][:, r : r + 1], bias=1.0)

        def square(h, r):
            row = ratio[h, r]
            if h == LAST:
                nc.vector.tensor_mul(out=row[:], in0=row[:], in1=row[:])
            else:
                nc.scalar.activation(out=row[:], in_=row[:], func=FUNC.Square)

        def exponential(h, r):
            e_bf[h, r] = work.tile([P, SEQ], BF16, name="e_bf")
            nc.scalar.activation(
                out=e_bf[h, r][:], in_=ratio[h, r][:, :SEQ], func=FUNC.Exp, scale=-1.0,
                bias=ratio[h, r][:, SEQ : SEQ + 1], accum_out=small[h]["rowsum"][:, r : r + 1],
            )
            e_flip[h, r] = flip_banks.tile([P, TILES, P], BF16, name="e_flip", tag="flip")
            for kt in range(TILES):
                nc.tensor.transpose(e_flip[h, r][:, kt, :], e_bf[h, r][:, kt * P : (kt + 1) * P], ident_b[:])

        def group(h, r):
            e_grp[h, r] = work.tile([P, PASSES, P, PACK], BF16, name="e_grp", align_bytes=64)
            copy_out = nc.vector.tensor_copy if h == LAST else nc.scalar.copy
            copy_out(out=e_grp[h, r][:], in_=e_flip[h, r][:].rearrange("p (g t) i -> p g i t", g=PASSES))

        def quantise_and_multiply(h, r):
            e_codes[h, r] = work.tile([P, PASSES * P], U32, name="e_codes", align_bytes=64)
            e_scales[h, r] = work.tile([P, PASSES * P], U8, name="e_scales", align_bytes=64)
            nc.vector.quantize_mx(
                out=e_codes[h, r][:].bitcast(FP8X4),
                scales=e_scales[h, r][:],
                in_=e_grp[h, r][:].rearrange("p g i t -> p (g i t)"),
            )
            nc.vector.reciprocal(out=small[h]["rinv"][:, r : r + 1], in_=small[h]["rowsum"][:, r : r + 1])
            pv[h, r] = out_banks.tile([P, FEAT], F32, name="pv")
            for g in range(PASSES):
                nc.tensor.matmul_mx(
                    out=pv[h, r][:],
                    lhsT=e_codes[h, r][:, g * P : (g + 1) * P].bitcast(FP8X4),
                    lhsT_scale=e_scales[h, r][:, g * P : (g + 1) * P],
                    rhs=v_codes[h][:, g, :].bitcast(FP8X4),
                    rhs_scale=v_scales[h][:, g, :],
                    start=(g == 0),
                    stop=(g == PASSES - 1),
                )

        def divide_and_store(h, r):
            result = work.tile([P, FEAT], F32, name="result")
            nc.scalar.activation(out=result[:], in_=pv[h, r][:], func=FUNC.Copy, scale=small[h]["rinv"][:, r : r + 1])
            nc.sync.dma_start(out=head_rows(out_rows, h).rearrange("(p r) d -> p r d", p=P)[:, r, :], in_=result[:])

        def exp_step(h, step):
            if step < TILES:
                exponential(h, step)
            if 0 <= step - 1 < TILES:
                group(h, step - 1)
            if 0 <= step - 2 < TILES:
                quantise_and_multiply(h, step - 2)
            if 0 <= step - 3 < TILES:
                divide_and_store(h, step - 3)

        load_qk(0)
        load_qk(1)
        load_qk(2)
        load_v(0)
        for step in range(TILES):
            norm(0, step, "kn")
            flip(0, step, nc.vector.tensor_copy)
        key_values(0)
        spread_keys(0)
        for step in range(TILES):
            norm(0, step, "qn")
        query_values(0)
        load_qk(3)
        for step in range(TILES):
            norm(1, step, "kn")
            norm(1, step, "qn")
        for x in range(BANKS + 2):
            score_step(0, x)
            if x < TILES:
                flip(1, x, nc.scalar.copy)
            if x < BANKS:
                norm(2 + x // TILES, x % TILES, "kn")
                norm(2 + x // TILES, x % TILES, "qn")
        for r in range(LEAD):
            multiply(0, r)

        for h in range(HEADS):
            for r in range(TILES):
                if h > 0 and r < 2:
                    score_step(h, BANKS + r)
                if r + LEAD < TILES:
                    multiply(h, r + LEAD)
                root(h, r)
                if h > 0 and r < CHAIN:
                    exp_step(h - 1, TILES + r)
                add_root(h, r)
                if h + 2 < HEADS:
                    flip(h + 2, r, nc.scalar.copy)

            if h + 1 < HEADS:
                key_values(h + 1)
            group_v(h)
            if h + 1 < HEADS:
                query_values(h + 1)
                spread_keys(h + 1)
            quantise_v(h)
            if h + 1 < HEADS:
                load_v(h + 1)

            for step in range(BANKS):
                if h + 1 < HEADS:
                    score_step(h + 1, step)
                if step < TILES:
                    logarithm(h, step)
                if 1 <= step <= TILES:
                    square(h, step - 1)
                if step >= TILES:
                    exp_step(h, step - TILES)
                if h + 1 < HEADS and step >= BANKS - LEAD:
                    multiply(h + 1, step - (BANKS - LEAD))

        for step in range(TILES, TILES + CHAIN):
            exp_step(LAST, step)
